import numpy as np
import ml_dtypes

BF16 = ml_dtypes.bfloat16


def bf(x):
    return np.asarray(x, np.float32).astype(BF16)


def f32(x):
    return np.asarray(x, np.float32)


def f64(x):
    return np.asarray(x).astype(np.float64)


def striped(idx):
    return np.tile(idx.reshape(-1, 16).T, (8, 1))


C, S, KN, D1, D2, D3, D4, D5, OUT, N = 384, 4096, 4, 2048, 1024, 512, 256, 128, 128, 8192


def dense(rows, cols):
    return bf(np.random.standard_normal((rows, cols)) / np.sqrt(rows))


def bias(rows):
    return f32(0.1 * np.random.standard_normal((rows, 1)))


def setup_inputs():
    return {
        "x": f32(np.random.standard_normal((C, S))),
        "w0": f32(np.random.standard_normal((1, N)) / np.sqrt(KN)),
        "b0": bias(D1),
        "w1": dense(D1, D2),
        "b1": bias(D2),
        "w2": dense(D2, D3),
        "b2": bias(D3),
        "w3": dense(D3, D4),
        "b3": bias(D4),
        "w4": dense(D4, D5),
        "b4": bias(D5),
        "fc_w": dense(D5, OUT),
        "fc_b": bias(OUT),
        "offs": striped(np.concatenate([np.random.permutation(S)[:D1] for _ in range(KN)])),
    }


def reference(x, w0, b0, w1, b1, w2, b2, w3, b3, w4, b4, fc_w, fc_b, offs):
    idx = offs[:16].T.reshape(-1)
    p = f64(x)[:, idx] * f64(w0)
    h = p.reshape(C, KN, D1).sum(axis=1) + f64(b0).T
    for w, b in ((w1, b1), (w2, b2), (w3, b3), (w4, b4)):
        h = h @ f64(w) + f64(b).T
    return h @ f64(fc_w) + f64(fc_b).T

@@ -1,0 +1,136 @@
+import concourse.mybir as mybir
+from concourse.masks import make_identity
+
+F32 = mybir.dt.float32
+BF16 = mybir.dt.bfloat16
+U16 = mybir.dt.uint16
+MULT = mybir.AluOpType.mult
+ADD = mybir.AluOpType.add
+IDENTITY = mybir.ActivationFunctionType.Identity
+
+P = 128
+C, S, KN = 384, 4096, 4
+D1, D2, D3, D4, D5, OUT = 2048, 1024, 512, 256, 128, 128
+N = KN * D1
+SAMPLE_BLOCKS = C // P
+CHUNK = 512
+CHUNKS = D1 // CHUNK
+BANK_BLOCKS = 4
+
+FLOPS = 2 * C * (N + D1 * D2 + D2 * D3 + D3 * D4 + D4 * D5 + D5 * OUT)
+
+
+def load_weights(nc, pool, name, w, rows_per_dma):
+    d_in, d_out = w.shape
+    tile = pool.tile([P, d_in // P, d_out], BF16, name=name)
+    view = w.rearrange("(j p) e -> p j e", p=P)
+    step = rows_per_dma // P
+    for j in range(0, d_in // P, step):
+        nc.sync.dma_start(tile[:, j : j + step, :], view[:, j : j + step, :])
+    return tile
+
+
+def load_bias(nc, pool, name, b):
+    tile = pool.tile([P, b.shape[0] // P], F32, name=name)
+    with nc.allow_non_contiguous_dma(reason="one float32 to a partition"):
+        nc.scalar.dma_start(tile[:], b.rearrange("(j p) o -> p (j o)", p=P))
+    return tile
+
+
+def dense_layer(nc, sums, acts, name, w_tile, b_tile, h_in):
+    blocks_in, d_out = w_tile.shape[1], w_tile.shape[2]
+    blocks_out = d_out // P
+    h_out = acts.tile([P, blocks_out, P], BF16, name=name)
+    for m0 in range(0, blocks_out, BANK_BLOCKS):
+        bank = range(m0, min(m0 + BANK_BLOCKS, blocks_out))
+        acc = sums.tile([P, BANK_BLOCKS, P], F32, name="acc")
+        for m in bank:
+            for j in range(blocks_in):
+                nc.tensor.matmul(
+                    acc[:, m - m0, :],
+                    lhsT=w_tile[:, j, m * P : (m + 1) * P],
+                    rhs=h_in[:, j, :],
+                    start=(j == 0),
+                    stop=(j == blocks_in - 1),
+                )
+        for m in bank:
+            nc.scalar.activation(h_out[:, m, :], acc[:, m - m0, :], IDENTITY, bias=b_tile[:, m : m + 1])
+    return h_out
+
+
+def tile_lcnspiking_b_kernel(tc, x, w0, b0, w1, b1, w2, b2, w3, b3, w4, b4, fc_w, fc_b, offs, out):
+    nc = tc.nc
+    with (
+        tc.tile_pool(name="held", bufs=1) as held,
+        tc.tile_pool(name="products", bufs=4) as products,
+        tc.tile_pool(name="acts", bufs=2) as acts,
+        tc.psum_pool(name="flipped", bufs=2) as flipped,
+        tc.psum_pool(name="sums", bufs=6) as sums,
+    ):
+        offsets = held.tile([P, N // 16], U16, name="offsets")
+        nc.sync.dma_start(offsets[:], offs)
+
+        w0_view = w0.rearrange("o (k c n) -> c o k n", k=KN, n=CHUNK)
+        w0_chunks = [held.tile([P, KN, CHUNK], F32, name="w0_chunk%d" % c) for c in range(CHUNKS)]
+        x_blocks = [held.tile([P, S], F32, name="x_block%d" % b) for b in range(SAMPLE_BLOCKS)]
+
+        nc.sync.dma_start(w0_chunks[0][:], w0_view[0, :, :, :].broadcast_to([P, KN, CHUNK]))
+        nc.sync.dma_start(x_blocks[0][:], x[0:P, :])
+        for c in range(1, CHUNKS):
+            nc.sync.dma_start(w0_chunks[c][:], w0_view[c, :, :, :].broadcast_to([P, KN, CHUNK]))
+        nc.sync.dma_start(x_blocks[1][:], x[P : 2 * P, :])
+        w1_tile = load_weights(nc, held, "w1_tile", w1, rows_per_dma=512)
+        nc.sync.dma_start(x_blocks[2][:], x[2 * P : 3 * P, :])
+        w2_tile = load_weights(nc, held, "w2_tile", w2, rows_per_dma=D2)
+        w3_tile = load_weights(nc, held, "w3_tile", w3, rows_per_dma=D3)
+        w4_tile = load_weights(nc, held, "w4_tile", w4, rows_per_dma=D4)
+        fcw_tile = load_weights(nc, held, "fcw_tile", fc_w, rows_per_dma=D5)
+
+        b0_tile = load_bias(nc, held, "b0_tile", b0)
+        b1_tile = load_bias(nc, held, "b1_tile", b1)
+        b2_tile = load_bias(nc, held, "b2_tile", b2)
+        b3_tile = load_bias(nc, held, "b3_tile", b3)
+        b4_tile = load_bias(nc, held, "b4_tile", b4)
+        fcb_rows = held.tile([P, OUT], F32, name="fcb_rows")
+        nc.scalar.dma_start(fcb_rows[:], fc_b.rearrange("e o -> o e").broadcast_to([P, OUT]))
+
+        identity = held.tile([P, P], F32, name="identity")
+        make_identity(nc, identity[:])
+
+        for b in range(SAMPLE_BLOCKS):
+            y0 = acts.tile([P, D1 // P, P], BF16, name="y0")
+            for c in range(CHUNKS):
+                prod = products.tile([P, KN, CHUNK], F32, name="prod")
+                for k in range(KN):
+                    first = (k * D1 + c * CHUNK) // 16
+                    nc.vector.tensor_tensor(
+                        prod[:, k, :],
+                        x_blocks[b][:].indirect(offsets[:, first : first + CHUNK // 16]),
+                        w0_chunks[c][:, k, :],
+                        MULT,
+                    )
+                y0_sum = flipped.tile([P, CHUNK // P, P], F32, name="y0_sum")
+                for i in range(CHUNK // P):
+                    for k in range(KN):
+                        nc.tensor.matmul(
+                            y0_sum[:, i, :],
+                            lhsT=prod[:, k, i * P : (i + 1) * P],
+                            rhs=identity[:],
+                            is_transpose=True,
+                            start=(k == 0),
+                            stop=(k == KN - 1),
+                        )
+                for i in range(CHUNK // P):
+                    j = c * (CHUNK // P) + i
+                    nc.scalar.activation(y0[:, j, :], y0_sum[:, i, :], IDENTITY, bias=b0_tile[:, j : j + 1])
+
+            h1 = dense_layer(nc, sums, acts, "h1", w1_tile, b1_tile, y0)
+            h2 = dense_layer(nc, sums, acts, "h2", w2_tile, b2_tile, h1)
+            h3 = dense_layer(nc, sums, acts, "h3", w3_tile, b3_tile, h2)
+            h4 = dense_layer(nc, sums, acts, "h4", w4_tile, b4_tile, h3)
+
+            out_sum = sums.tile([P, BANK_BLOCKS, P], F32, name="acc")
+            nc.tensor.matmul(out_sum[:, 0, :], lhsT=h4[:, 0, :], rhs=fcw_tile[:, 0, :], start=True, stop=True)
+            out_rows = acts.tile([P, OUT], F32, name="out_rows")
+            nc.vector.tensor_tensor(out_rows[:], out_sum[:, 0, :], fcb_rows[:], ADD)
+            nc.sync.dma_start(out[b * P : (b + 1) * P, :], out_rows[:])

@@ -20,14 +20,17 @@ BANK_BLOCKS = 4
 FLOPS = 2 * C * (N + D1 * D2 + D2 * D3 + D3 * D4 + D4 * D5 + D5 * OUT)
 
 
-def load_weights(nc, pool, name, w, rows_per_dma):
-    d_in, d_out = w.shape
-    tile = pool.tile([P, d_in // P, d_out], BF16, name=name)
-    view = w.rearrange("(j p) e -> p j e", p=P)
-    step = rows_per_dma // P
-    for j in range(0, d_in // P, step):
-        nc.sync.dma_start(tile[:, j : j + step, :], view[:, j : j + step, :])
-    return tile
+def weight_tile(pool, name, w):
+    return pool.tile([P, w.shape[0] // P, w.shape[1]], BF16, name=name)
+
+
+def load_blocks(nc, w_tile, w, j0, j1):
+    nc.sync.dma_start(w_tile[:, j0:j1, :], w.rearrange("(j p) e -> p j e", p=P)[:, j0:j1, :])
+
+
+def load_w0(nc, w0_chunks, w0, c, k):
+    first = k * D1 + c * CHUNK
+    nc.sync.dma_start(w0_chunks[c][:, k, :], w0[0:1, first : first + CHUNK].broadcast_to([P, CHUNK]))
 
 
 def load_bias(nc, pool, name, b):
@@ -37,25 +40,40 @@ def load_bias(nc, pool, name, b):
     return tile
 
 
-def dense_layer(nc, sums, acts, name, w_tile, b_tile, h_in):
-    blocks_in, d_out = w_tile.shape[1], w_tile.shape[2]
-    blocks_out = d_out // P
+def open_banks(sums, w_tile):
+    blocks_out = w_tile.shape[2] // P
+    return [sums.tile([P, BANK_BLOCKS, P], F32, name="acc") for m0 in range(0, blocks_out, BANK_BLOCKS)]
+
+
+def add_block(nc, banks, w_tile, h_in, j):
+    blocks_in, blocks_out = w_tile.shape[1], w_tile.shape[2] // P
+    for m in range(blocks_out):
+        place = m % BANK_BLOCKS
+        last_of_bank = place == BANK_BLOCKS - 1 or m == blocks_out - 1
+        nc.tensor.matmul(
+            banks[m // BANK_BLOCKS][:, place, :],
+            lhsT=w_tile[:, j, m * P : (m + 1) * P],
+            rhs=h_in[:, j, :],
+            start=(j == 0 and place == 0),
+            stop=(j == blocks_in - 1 and last_of_bank),
+        )
+
+
+def add_bias(nc, acts, name, banks, b_tile):
+    blocks_out = b_tile.shape[1]
     h_out = acts.tile([P, blocks_out, P], BF16, name=name)
-    for m0 in range(0, blocks_out, BANK_BLOCKS):
-        bank = range(m0, min(m0 + BANK_BLOCKS, blocks_out))
-        acc = sums.tile([P, BANK_BLOCKS, P], F32, name="acc")
-        for m in bank:
-            for j in range(blocks_in):
-                nc.tensor.matmul(
-                    acc[:, m - m0, :],
-                    lhsT=w_tile[:, j, m * P : (m + 1) * P],
-                    rhs=h_in[:, j, :],
-                    start=(j == 0),
-                    stop=(j == blocks_in - 1),
-                )
-        for m in bank:
-            nc.scalar.activation(h_out[:, m, :], acc[:, m - m0, :], IDENTITY, bias=b_tile[:, m : m + 1])
+    for m in range(blocks_out):
+        nc.scalar.activation(
+            h_out[:, m, :], banks[m // BANK_BLOCKS][:, m % BANK_BLOCKS, :], IDENTITY, bias=b_tile[:, m : m + 1]
+        )
     return h_out
+
+
+def dense_layer(nc, sums, acts, name, w_tile, b_tile, h_in):
+    banks = open_banks(sums, w_tile)
+    for j in range(w_tile.shape[1]):
+        add_block(nc, banks, w_tile, h_in, j)
+    return add_bias(nc, acts, name, banks, b_tile)
 
 
 def tile_lcnspiking_b_kernel(tc, x, w0, b0, w1, b1, w2, b2, w3, b3, w4, b4, fc_w, fc_b, offs, out):
@@ -70,21 +88,32 @@ def tile_lcnspiking_b_kernel(tc, x, w0, b0, w1, b1, w2, b2, w3, b3, w4, b4, fc_w
         offsets = held.tile([P, N // 16], U16, name="offsets")
         nc.sync.dma_start(offsets[:], offs)
 
-        w0_view = w0.rearrange("o (k c n) -> c o k n", k=KN, n=CHUNK)
         w0_chunks = [held.tile([P, KN, CHUNK], F32, name="w0_chunk%d" % c) for c in range(CHUNKS)]
         x_blocks = [held.tile([P, S], F32, name="x_block%d" % b) for b in range(SAMPLE_BLOCKS)]
 
-        nc.sync.dma_start(w0_chunks[0][:], w0_view[0, :, :, :].broadcast_to([P, KN, CHUNK]))
+        w1_tile = weight_tile(held, "w1_tile", w1)
+        w2_tile = weight_tile(held, "w2_tile", w2)
+        w3_tile = weight_tile(held, "w3_tile", w3)
+        w4_tile = weight_tile(held, "w4_tile", w4)
+        fcw_tile = weight_tile(held, "fcw_tile", fc_w)
+
+        load_w0(nc, w0_chunks, w0, 0, 0)
         nc.sync.dma_start(x_blocks[0][:], x[0:P, :])
+        for k in range(1, KN):
+            load_w0(nc, w0_chunks, w0, 0, k)
         for c in range(1, CHUNKS):
-            nc.sync.dma_start(w0_chunks[c][:], w0_view[c, :, :, :].broadcast_to([P, KN, CHUNK]))
+            for k in range(KN):
+                load_w0(nc, w0_chunks, w0, c, k)
+        load_blocks(nc, w1_tile, w1, 0, 4)
+        load_blocks(nc, w1_tile, w1, 4, 8)
         nc.sync.dma_start(x_blocks[1][:], x[P : 2 * P, :])
-        w1_tile = load_weights(nc, held, "w1_tile", w1, rows_per_dma=512)
+        load_blocks(nc, w1_tile, w1, 8, 12)
+        load_blocks(nc, w1_tile, w1, 12, 16)
+        load_blocks(nc, w2_tile, w2, 0, D2 // P)
+        load_blocks(nc, w3_tile, w3, 0, D3 // P)
+        load_blocks(nc, w4_tile, w4, 0, D4 // P)
+        load_blocks(nc, fcw_tile, fc_w, 0, D5 // P)
         nc.sync.dma_start(x_blocks[2][:], x[2 * P : 3 * P, :])
-        w2_tile = load_weights(nc, held, "w2_tile", w2, rows_per_dma=D2)
-        w3_tile = load_weights(nc, held, "w3_tile", w3, rows_per_dma=D3)
-        w4_tile = load_weights(nc, held, "w4_tile", w4, rows_per_dma=D4)
-        fcw_tile = load_weights(nc, held, "fcw_tile", fc_w, rows_per_dma=D5)
 
         b0_tile = load_bias(nc, held, "b0_tile", b0)
         b1_tile = load_bias(nc, held, "b1_tile", b1)
@@ -99,6 +128,7 @@ def tile_lcnspiking_b_kernel(tc, x, w0, b0, w1, b1, w2, b2, w3, b3, w4, b4, fc_w
 
         for b in range(SAMPLE_BLOCKS):
             y0 = acts.tile([P, D1 // P, P], BF16, name="y0")
+            h1_banks = open_banks(sums, w1_tile)
             for c in range(CHUNKS):
                 prod = products.tile([P, KN, CHUNK], F32, name="prod")
                 for k in range(KN):
@@ -123,8 +153,10 @@ def tile_lcnspiking_b_kernel(tc, x, w0, b0, w1, b1, w2, b2, w3, b3, w4, b4, fc_w
                 for i in range(CHUNK // P):
                     j = c * (CHUNK // P) + i
                     nc.scalar.activation(y0[:, j, :], y0_sum[:, i, :], IDENTITY, bias=b0_tile[:, j : j + 1])
+                for i in range(CHUNK // P):
+                    add_block(nc, h1_banks, w1_tile, y0, c * (CHUNK // P) + i)
 
-            h1 = dense_layer(nc, sums, acts, "h1", w1_tile, b1_tile, y0)
+            h1 = add_bias(nc, acts, "h1", h1_banks, b1_tile)
             h2 = dense_layer(nc, sums, acts, "h2", w2_tile, b2_tile, h1)
             h3 = dense_layer(nc, sums, acts, "h3", w3_tile, b3_tile, h2)
             h4 = dense_layer(nc, sums, acts, "h4", w4_tile, b4_tile, h3)

@@ -13,11 +13,24 @@ C, S, KN = 384, 4096, 4
 D1, D2, D3, D4, D5, OUT = 2048, 1024, 512, 256, 128, 128
 N = KN * D1
 SAMPLE_BLOCKS = C // P
-CHUNK = 512
-CHUNKS = D1 // CHUNK
 BANK_BLOCKS = 4
 
+PIECE = 512
+STEP = PIECE // KN
+PIECES = KN * (D1 // PIECE) + KN - 1
+
 FLOPS = 2 * C * (N + D1 * D2 + D2 * D3 + D3 * D4 + D4 * D5 + D5 * OUT)
+
+
+def piece_of(s):
+    k, turn = s % KN, s // KN
+    cut = turn * PIECE + (k + 1) * STEP
+    return k, max(cut - PIECE, 0), min(cut, D1)
+
+
+def load_w0(nc, w0_rows, w0, s):
+    k, lo, hi = piece_of(s)
+    nc.sync.dma_start(w0_rows[:, k, lo:hi], w0[0:1, k * D1 + lo : k * D1 + hi].broadcast_to([P, hi - lo]))
 
 
 def weight_tile(pool, name, w):
@@ -28,21 +41,26 @@ def load_blocks(nc, w_tile, w, j0, j1):
     nc.sync.dma_start(w_tile[:, j0:j1, :], w.rearrange("(j p) e -> p j e", p=P)[:, j0:j1, :])
 
 
-def load_w0(nc, w0_chunks, w0, c, k):
-    first = k * D1 + c * CHUNK
-    nc.sync.dma_start(w0_chunks[c][:, k, :], w0[0:1, first : first + CHUNK].broadcast_to([P, CHUNK]))
+def load_biases(nc, held, flipped, identity, biases):
+    rows = held.tile([P, P], F32, name="bias_rows")
+    nc.gpsimd.memset(rows[:], 0.0)
+    first_row = []
+    used = 0
+    for b in biases:
+        first_row.append(used)
+        blocks = b.shape[0] // P
+        nc.scalar.dma_start(rows[used : used + blocks, :], b.rearrange("(j p) o -> j (p o)", p=P))
+        used += blocks
+    turned = flipped.tile([P, P], F32, name="y0_sum")
+    nc.tensor.transpose(turned[:], rows[:], identity[:])
+    columns = held.tile([P, P], F32, name="bias_columns")
+    nc.scalar.activation(columns[:], turned[:], IDENTITY)
+    return [columns[:, r : r + b.shape[0] // P] for r, b in zip(first_row, biases)]
 
 
-def load_bias(nc, pool, name, b):
-    tile = pool.tile([P, b.shape[0] // P], F32, name=name)
-    with nc.allow_non_contiguous_dma(reason="one float32 to a partition"):
-        nc.scalar.dma_start(tile[:], b.rearrange("(j p) o -> p (j o)", p=P))
-    return tile
-
-
-def open_banks(sums, w_tile):
+def open_banks(psum, w_tile):
     blocks_out = w_tile.shape[2] // P
-    return [sums.tile([P, BANK_BLOCKS, P], F32, name="acc") for m0 in range(0, blocks_out, BANK_BLOCKS)]
+    return [psum.tile([P, BANK_BLOCKS, P], F32, name="acc") for m0 in range(0, blocks_out, BANK_BLOCKS)]
 
 
 def add_block(nc, banks, w_tile, h_in, j):
@@ -69,8 +87,8 @@ def add_bias(nc, acts, name, banks, b_tile):
     return h_out
 
 
-def dense_layer(nc, sums, acts, name, w_tile, b_tile, h_in):
-    banks = open_banks(sums, w_tile)
+def dense_layer(nc, psum, acts, name, w_tile, b_tile, h_in):
+    banks = open_banks(psum, w_tile)
     for j in range(w_tile.shape[1]):
         add_block(nc, banks, w_tile, h_in, j)
     return add_bias(nc, acts, name, banks, b_tile)
@@ -80,88 +98,80 @@ def tile_lcnspiking_b_kernel(tc, x, w0, b0, w1, b1, w2, b2, w3, b3, w4, b4, fc_w
     nc = tc.nc
     with (
         tc.tile_pool(name="held", bufs=1) as held,
-        tc.tile_pool(name="products", bufs=4) as products,
+        tc.tile_pool(name="products", bufs=2) as products,
         tc.tile_pool(name="acts", bufs=2) as acts,
         tc.psum_pool(name="flipped", bufs=2) as flipped,
-        tc.psum_pool(name="sums", bufs=6) as sums,
+        tc.psum_pool(name="wide", bufs=4) as wide,
+        tc.psum_pool(name="narrow", bufs=2) as narrow,
     ):
         offsets = held.tile([P, N // 16], U16, name="offsets")
         nc.sync.dma_start(offsets[:], offs)
 
-        w0_chunks = [held.tile([P, KN, CHUNK], F32, name="w0_chunk%d" % c) for c in range(CHUNKS)]
+        w0_rows = held.tile([P, KN, D1], F32, name="w0_rows")
         x_blocks = [held.tile([P, S], F32, name="x_block%d" % b) for b in range(SAMPLE_BLOCKS)]
-
         w1_tile = weight_tile(held, "w1_tile", w1)
         w2_tile = weight_tile(held, "w2_tile", w2)
         w3_tile = weight_tile(held, "w3_tile", w3)
         w4_tile = weight_tile(held, "w4_tile", w4)
         fcw_tile = weight_tile(held, "fcw_tile", fc_w)
 
-        load_w0(nc, w0_chunks, w0, 0, 0)
+        load_w0(nc, w0_rows, w0, 0)
         nc.sync.dma_start(x_blocks[0][:], x[0:P, :])
-        for k in range(1, KN):
-            load_w0(nc, w0_chunks, w0, 0, k)
-        for c in range(1, CHUNKS):
-            for k in range(KN):
-                load_w0(nc, w0_chunks, w0, c, k)
-        load_blocks(nc, w1_tile, w1, 0, 4)
-        load_blocks(nc, w1_tile, w1, 4, 8)
+        for s in range(1, PIECES):
+            load_w0(nc, w0_rows, w0, s)
+            if s >= 2 * KN - 1 and s % KN == KN - 1:
+                j0 = (s // KN - 1) * (PIECE // P)
+                load_blocks(nc, w1_tile, w1, j0, j0 + PIECE // P)
         nc.sync.dma_start(x_blocks[1][:], x[P : 2 * P, :])
-        load_blocks(nc, w1_tile, w1, 8, 12)
-        load_blocks(nc, w1_tile, w1, 12, 16)
+        load_blocks(nc, w1_tile, w1, (D1 - PIECE) // P, D1 // P)
         load_blocks(nc, w2_tile, w2, 0, D2 // P)
         load_blocks(nc, w3_tile, w3, 0, D3 // P)
         load_blocks(nc, w4_tile, w4, 0, D4 // P)
         load_blocks(nc, fcw_tile, fc_w, 0, D5 // P)
-        nc.sync.dma_start(x_blocks[2][:], x[2 * P : 3 * P, :])
-
-        b0_tile = load_bias(nc, held, "b0_tile", b0)
-        b1_tile = load_bias(nc, held, "b1_tile", b1)
-        b2_tile = load_bias(nc, held, "b2_tile", b2)
-        b3_tile = load_bias(nc, held, "b3_tile", b3)
-        b4_tile = load_bias(nc, held, "b4_tile", b4)
         fcb_rows = held.tile([P, OUT], F32, name="fcb_rows")
-        nc.scalar.dma_start(fcb_rows[:], fc_b.rearrange("e o -> o e").broadcast_to([P, OUT]))
+        nc.sync.dma_start(fcb_rows[:], fc_b.rearrange("e o -> o e").broadcast_to([P, OUT]))
+        nc.sync.dma_start(x_blocks[2][:], x[2 * P : 3 * P, :])
 
         identity = held.tile([P, P], F32, name="identity")
         make_identity(nc, identity[:])
+        b0_tile, b1_tile, b2_tile, b3_tile, b4_tile = load_biases(nc, held, flipped, identity, [b0, b1, b2, b3, b4])
 
         for b in range(SAMPLE_BLOCKS):
+            prod = products.tile([P, KN, D1], F32, name="prod")
             y0 = acts.tile([P, D1 // P, P], BF16, name="y0")
-            h1_banks = open_banks(sums, w1_tile)
-            for c in range(CHUNKS):
-                prod = products.tile([P, KN, CHUNK], F32, name="prod")
-                for k in range(KN):
-                    first = (k * D1 + c * CHUNK) // 16
-                    nc.vector.tensor_tensor(
-                        prod[:, k, :],
-                        x_blocks[b][:].indirect(offsets[:, first : first + CHUNK // 16]),
-                        w0_chunks[c][:, k, :],
-                        MULT,
-                    )
-                y0_sum = flipped.tile([P, CHUNK // P, P], F32, name="y0_sum")
-                for i in range(CHUNK // P):
+            h1_banks = open_banks(wide, w1_tile)
+            for s in range(PIECES):
+                k, lo, hi = piece_of(s)
+                first = (k * D1 + lo) // 16
+                nc.vector.tensor_tensor(
+                    prod[:, k, lo:hi],
+                    x_blocks[b][:].indirect(offsets[:, first : first + (hi - lo) // 16]),
+                    w0_rows[:, k, lo:hi],
+                    MULT,
+                )
+                if s < KN - 1:
+                    continue
+                done = (s - (KN - 1)) * STEP // P
+                for j in range(done, done + STEP // P):
+                    y0_sum = flipped.tile([P, P], F32, name="y0_sum")
                     for k in range(KN):
                         nc.tensor.matmul(
-                            y0_sum[:, i, :],
-                            lhsT=prod[:, k, i * P : (i + 1) * P],
+                            y0_sum[:],
+                            lhsT=prod[:, k, j * P : (j + 1) * P],
                             rhs=identity[:],
                             is_transpose=True,
                             start=(k == 0),
                             stop=(k == KN - 1),
                         )
-                for i in range(CHUNK // P):
-                    j = c * (CHUNK // P) + i
-                    nc.scalar.activation(y0[:, j, :], y0_sum[:, i, :], IDENTITY, bias=b0_tile[:, j : j + 1])
-                for i in range(CHUNK // P):
-                    add_block(nc, h1_banks, w1_tile, y0, c * (CHUNK // P) + i)
+                    nc.scalar.activation(y0[:, j, :], y0_sum[:], IDENTITY, bias=b0_tile[:, j : j + 1])
+                    add_block(nc, h1_banks, w1_tile, y0, j)
 
             h1 = add_bias(nc, acts, "h1", h1_banks, b1_tile)
-            h2 = dense_layer(nc, sums, acts, "h2", w2_tile, b2_tile, h1)
-            h3 = dense_layer(nc, sums, acts, "h3", w3_tile, b3_tile, h2)
-            h4 = dense_layer(nc, sums, acts, "h4", w4_tile, b4_tile, h3)
+            h2 = dense_layer(nc, narrow, acts, "h2", w2_tile, b2_tile, h1)
+            h3 = dense_layer(nc, narrow, acts, "h3", w3_tile, b3_tile, h2)
+            h4 = dense_layer(nc, narrow, acts, "h4", w4_tile, b4_tile, h3)
 
-            out_sum = sums.tile([P, BANK_BLOCKS, P], F32, name="acc")
+            out_sum = narrow.tile([P, BANK_BLOCKS, P], F32, name="acc")
             nc.tensor.matmul(out_sum[:, 0, :], lhsT=h4[:, 0, :], rhs=fcw_tile[:, 0, :], start=True, stop=True)
             out_rows = acts.tile([P, OUT], F32, name="out_rows")
             nc.vector.tensor_tensor(out_rows[:], out_sum[:, 0, :], fcb_rows[:], ADD)

@@ -13,24 +13,11 @@ C, S, KN = 384, 4096, 4
 D1, D2, D3, D4, D5, OUT = 2048, 1024, 512, 256, 128, 128
 N = KN * D1
 SAMPLE_BLOCKS = C // P
+CHUNK = 512
+CHUNKS = D1 // CHUNK
 BANK_BLOCKS = 4
 
-PIECE = 512
-STEP = PIECE // KN
-PIECES = KN * (D1 // PIECE) + KN - 1
-
 FLOPS = 2 * C * (N + D1 * D2 + D2 * D3 + D3 * D4 + D4 * D5 + D5 * OUT)
-
-
-def piece_of(s):
-    k, turn = s % KN, s // KN
-    cut = turn * PIECE + (k + 1) * STEP
-    return k, max(cut - PIECE, 0), min(cut, D1)
-
-
-def load_w0(nc, w0_rows, w0, s):
-    k, lo, hi = piece_of(s)
-    nc.sync.dma_start(w0_rows[:, k, lo:hi], w0[0:1, k * D1 + lo : k * D1 + hi].broadcast_to([P, hi - lo]))
 
 
 def weight_tile(pool, name, w):
@@ -39,6 +26,11 @@ def weight_tile(pool, name, w):
 
 def load_blocks(nc, w_tile, w, j0, j1):
     nc.sync.dma_start(w_tile[:, j0:j1, :], w.rearrange("(j p) e -> p j e", p=P)[:, j0:j1, :])
+
+
+def load_w0(nc, w0_chunks, w0, c, k):
+    first = k * D1 + c * CHUNK
+    nc.sync.dma_start(w0_chunks[c][:, k, :], w0[0:1, first : first + CHUNK].broadcast_to([P, CHUNK]))
 
 
 def load_biases(nc, held, flipped, identity, biases):
@@ -51,16 +43,16 @@ def load_biases(nc, held, flipped, identity, biases):
         blocks = b.shape[0] // P
         nc.scalar.dma_start(rows[used : used + blocks, :], b.rearrange("(j p) o -> j (p o)", p=P))
         used += blocks
-    turned = flipped.tile([P, P], F32, name="y0_sum")
-    nc.tensor.transpose(turned[:], rows[:], identity[:])
+    turned = flipped.tile([P, CHUNK // P, P], F32, name="y0_sum")
+    nc.tensor.transpose(turned[:, 0, :], rows[:], identity[:])
     columns = held.tile([P, P], F32, name="bias_columns")
-    nc.scalar.activation(columns[:], turned[:], IDENTITY)
+    nc.scalar.activation(columns[:], turned[:, 0, :], IDENTITY)
     return [columns[:, r : r + b.shape[0] // P] for r, b in zip(first_row, biases)]
 
 
-def open_banks(psum, w_tile):
+def open_banks(sums, w_tile):
     blocks_out = w_tile.shape[2] // P
-    return [psum.tile([P, BANK_BLOCKS, P], F32, name="acc") for m0 in range(0, blocks_out, BANK_BLOCKS)]
+    return [sums.tile([P, BANK_BLOCKS, P], F32, name="acc") for m0 in range(0, blocks_out, BANK_BLOCKS)]
 
 
 def add_block(nc, banks, w_tile, h_in, j):
@@ -87,8 +79,8 @@ def add_bias(nc, acts, name, banks, b_tile):
     return h_out
 
 
-def dense_layer(nc, psum, acts, name, w_tile, b_tile, h_in):
-    banks = open_banks(psum, w_tile)
+def dense_layer(nc, sums, acts, name, w_tile, b_tile, h_in):
+    banks = open_banks(sums, w_tile)
     for j in range(w_tile.shape[1]):
         add_block(nc, banks, w_tile, h_in, j)
     return add_bias(nc, acts, name, banks, b_tile)
@@ -98,32 +90,35 @@ def tile_lcnspiking_b_kernel(tc, x, w0, b0, w1, b1, w2, b2, w3, b3, w4, b4, fc_w
     nc = tc.nc
     with (
         tc.tile_pool(name="held", bufs=1) as held,
-        tc.tile_pool(name="products", bufs=2) as products,
+        tc.tile_pool(name="products", bufs=4) as products,
         tc.tile_pool(name="acts", bufs=2) as acts,
         tc.psum_pool(name="flipped", bufs=2) as flipped,
-        tc.psum_pool(name="wide", bufs=4) as wide,
-        tc.psum_pool(name="narrow", bufs=2) as narrow,
+        tc.psum_pool(name="sums", bufs=6) as sums,
     ):
         offsets = held.tile([P, N // 16], U16, name="offsets")
         nc.sync.dma_start(offsets[:], offs)
 
-        w0_rows = held.tile([P, KN, D1], F32, name="w0_rows")
+        w0_chunks = [held.tile([P, KN, CHUNK], F32, name="w0_chunk%d" % c) for c in range(CHUNKS)]
         x_blocks = [held.tile([P, S], F32, name="x_block%d" % b) for b in range(SAMPLE_BLOCKS)]
+
         w1_tile = weight_tile(held, "w1_tile", w1)
         w2_tile = weight_tile(held, "w2_tile", w2)
         w3_tile = weight_tile(held, "w3_tile", w3)
         w4_tile = weight_tile(held, "w4_tile", w4)
         fcw_tile = weight_tile(held, "fcw_tile", fc_w)
 
-        load_w0(nc, w0_rows, w0, 0)
+        load_w0(nc, w0_chunks, w0, 0, 0)
         nc.sync.dma_start(x_blocks[0][:], x[0:P, :])
-        for s in range(1, PIECES):
-            load_w0(nc, w0_rows, w0, s)
-            if s >= 2 * KN - 1 and s % KN == KN - 1:
-                j0 = (s // KN - 1) * (PIECE // P)
-                load_blocks(nc, w1_tile, w1, j0, j0 + PIECE // P)
+        for k in range(1, KN):
+            load_w0(nc, w0_chunks, w0, 0, k)
+        for c in range(1, CHUNKS):
+            for k in range(KN):
+                load_w0(nc, w0_chunks, w0, c, k)
+        load_blocks(nc, w1_tile, w1, 0, 4)
+        load_blocks(nc, w1_tile, w1, 4, 8)
         nc.sync.dma_start(x_blocks[1][:], x[P : 2 * P, :])
-        load_blocks(nc, w1_tile, w1, (D1 - PIECE) // P, D1 // P)
+        load_blocks(nc, w1_tile, w1, 8, 12)
+        load_blocks(nc, w1_tile, w1, 12, 16)
         load_blocks(nc, w2_tile, w2, 0, D2 // P)
         load_blocks(nc, w3_tile, w3, 0, D3 // P)
         load_blocks(nc, w4_tile, w4, 0, D4 // P)
@@ -137,41 +132,41 @@ def tile_lcnspiking_b_kernel(tc, x, w0, b0, w1, b1, w2, b2, w3, b3, w4, b4, fc_w
         b0_tile, b1_tile, b2_tile, b3_tile, b4_tile = load_biases(nc, held, flipped, identity, [b0, b1, b2, b3, b4])
 
         for b in range(SAMPLE_BLOCKS):
-            prod = products.tile([P, KN, D1], F32, name="prod")
             y0 = acts.tile([P, D1 // P, P], BF16, name="y0")
-            h1_banks = open_banks(wide, w1_tile)
-            for s in range(PIECES):
-                k, lo, hi = piece_of(s)
-                first = (k * D1 + lo) // 16
-                nc.vector.tensor_tensor(
-                    prod[:, k, lo:hi],
-                    x_blocks[b][:].indirect(offsets[:, first : first + (hi - lo) // 16]),
-                    w0_rows[:, k, lo:hi],
-                    MULT,
-                )
-                if s < KN - 1:
-                    continue
-                done = (s - (KN - 1)) * STEP // P
-                for j in range(done, done + STEP // P):
-                    y0_sum = flipped.tile([P, P], F32, name="y0_sum")
-                    for k in range(KN):
+            h1_banks = open_banks(sums, w1_tile)
+            for c in range(CHUNKS):
+                prod = products.tile([P, KN, CHUNK], F32, name="prod")
+                for k in range(KN):
+                    first = (k * D1 + c * CHUNK) // 16
+                    nc.vector.tensor_tensor(
+                        prod[:, k, :],
+                        x_blocks[b][:].indirect(offsets[:, first : first + CHUNK // 16]),
+                        w0_chunks[c][:, k, :],
+                        MULT,
+                    )
+                y0_sum = flipped.tile([P, CHUNK // P, P], F32, name="y0_sum")
+                for k in range(KN):
+                    for i in range(CHUNK // P):
                         nc.tensor.matmul(
-                            y0_sum[:],
-                            lhsT=prod[:, k, j * P : (j + 1) * P],
+                            y0_sum[:, i, :],
+                            lhsT=prod[:, k, i * P : (i + 1) * P],
                             rhs=identity[:],
                             is_transpose=True,
-                            start=(k == 0),
-                            stop=(k == KN - 1),
+                            start=(k == 0 and i == 0),
+                            stop=(k == KN - 1 and i == CHUNK // P - 1),
                         )
-                    nc.scalar.activation(y0[:, j, :], y0_sum[:], IDENTITY, bias=b0_tile[:, j : j + 1])
-                    add_block(nc, h1_banks, w1_tile, y0, j)
+                for i in range(CHUNK // P):
+                    j = c * (CHUNK // P) + i
+                    nc.scalar.activation(y0[:, j, :], y0_sum[:, i, :], IDENTITY, bias=b0_tile[:, j : j + 1])
+                for i in range(CHUNK // P):
+                    add_block(nc, h1_banks, w1_tile, y0, c * (CHUNK // P) + i)
 
             h1 = add_bias(nc, acts, "h1", h1_banks, b1_tile)
-            h2 = dense_layer(nc, narrow, acts, "h2", w2_tile, b2_tile, h1)
-            h3 = dense_layer(nc, narrow, acts, "h3", w3_tile, b3_tile, h2)
-            h4 = dense_layer(nc, narrow, acts, "h4", w4_tile, b4_tile, h3)
+            h2 = dense_layer(nc, sums, acts, "h2", w2_tile, b2_tile, h1)
+            h3 = dense_layer(nc, sums, acts, "h3", w3_tile, b3_tile, h2)
+            h4 = dense_layer(nc, sums, acts, "h4", w4_tile, b4_tile, h3)
 
-            out_sum = narrow.tile([P, BANK_BLOCKS, P], F32, name="acc")
+            out_sum = sums.tile([P, BANK_BLOCKS, P], F32, name="acc")
             nc.tensor.matmul(out_sum[:, 0, :], lhsT=h4[:, 0, :], rhs=fcw_tile[:, 0, :], start=True, stop=True)
             out_rows = acts.tile([P, OUT], F32, name="out_rows")
             nc.vector.tensor_tensor(out_rows[:], out_sum[:, 0, :], fcb_rows[:], ADD)

@@ -28,26 +28,30 @@ def load_blocks(nc, w_tile, w, j0, j1):
     nc.sync.dma_start(w_tile[:, j0:j1, :], w.rearrange("(j p) e -> p j e", p=P)[:, j0:j1, :])
 
 
-def load_w0(nc, w0_chunks, w0, c, k):
-    first = k * D1 + c * CHUNK
-    nc.sync.dma_start(w0_chunks[c][:, k, :], w0[0:1, first : first + CHUNK].broadcast_to([P, CHUNK]))
-
-
-def load_biases(nc, held, flipped, identity, biases):
-    rows = held.tile([P, P], F32, name="bias_rows")
-    nc.gpsimd.memset(rows[:], 0.0)
-    first_row = []
+def load_bias_rows(nc, rows, biases):
     used = 0
     for b in biases:
-        first_row.append(used)
         blocks = b.shape[0] // P
-        nc.scalar.dma_start(rows[used : used + blocks, :], b.rearrange("(j p) o -> j (p o)", p=P))
+        nc.sync.dma_start(rows[used : used + blocks, :], b.rearrange("(j p) o -> j (p o)", p=P))
         used += blocks
-    turned = flipped.tile([P, CHUNK // P, P], F32, name="y0_sum")
-    nc.tensor.transpose(turned[:, 0, :], rows[:], identity[:])
-    columns = held.tile([P, P], F32, name="bias_columns")
-    nc.scalar.activation(columns[:], turned[:, 0, :], IDENTITY)
-    return [columns[:, r : r + b.shape[0] // P] for r, b in zip(first_row, biases)]
+
+
+def turn_rows(nc, held, flipped, identity, name, rows):
+    count = rows.shape[0]
+    turned = flipped.tile([P, CHUNK], F32, name="turned", tag="bank")
+    nc.tensor.transpose(turned[:, 0:count], rows[:], identity[0:count, 0:count])
+    columns = held.tile([P, count], F32, name=name)
+    nc.scalar.activation(columns[:], turned[:, 0:count], IDENTITY)
+    return columns
+
+
+def spread(nc, flipped, identity, columns, first, out_rows):
+    width = out_rows.shape[1]
+    repeated = flipped.tile([P, CHUNK], F32, name="repeated", tag="bank")
+    for i in range(width // P):
+        column = columns[:, first + i : first + i + 1]
+        nc.tensor.transpose(repeated[:, i * P : (i + 1) * P], column.to_broadcast([P, P]), identity[:])
+    nc.scalar.activation(out_rows, repeated[:, 0:width], IDENTITY)
 
 
 def open_banks(sums, w_tile):
@@ -92,9 +96,11 @@ def tile_lcnspiking_b_kernel(tc, x, w0, b0, w1, b1, w2, b2, w3, b3, w4, b4, fc_w
         tc.tile_pool(name="held", bufs=1) as held,
         tc.tile_pool(name="products", bufs=4) as products,
         tc.tile_pool(name="acts", bufs=2) as acts,
-        tc.psum_pool(name="flipped", bufs=2) as flipped,
-        tc.psum_pool(name="sums", bufs=6) as sums,
+        tc.psum_pool(name="flipped", bufs=3) as flipped,
+        tc.psum_pool(name="sums", bufs=5) as sums,
     ):
+        w0_rows = held.tile([N // P, P], F32, name="w0_rows")
+        nc.sync.dma_start(w0_rows[:], w0.rearrange("o (q n) -> (o q) n", n=P))
         offsets = held.tile([P, N // 16], U16, name="offsets")
         nc.sync.dma_start(offsets[:], offs)
 
@@ -107,13 +113,11 @@ def tile_lcnspiking_b_kernel(tc, x, w0, b0, w1, b1, w2, b2, w3, b3, w4, b4, fc_w
         w4_tile = weight_tile(held, "w4_tile", w4)
         fcw_tile = weight_tile(held, "fcw_tile", fc_w)
 
-        load_w0(nc, w0_chunks, w0, 0, 0)
         nc.sync.dma_start(x_blocks[0][:], x[0:P, :])
-        for k in range(1, KN):
-            load_w0(nc, w0_chunks, w0, 0, k)
-        for c in range(1, CHUNKS):
-            for k in range(KN):
-                load_w0(nc, w0_chunks, w0, c, k)
+        biases = [b0, b1, b2, b3, b4, fc_b]
+        bias_rows = held.tile([P, P], F32, name="bias_rows")
+        nc.gpsimd.memset(bias_rows[:], 0.0)
+        load_bias_rows(nc, bias_rows, biases)
         load_blocks(nc, w1_tile, w1, 0, 4)
         load_blocks(nc, w1_tile, w1, 4, 8)
         nc.sync.dma_start(x_blocks[1][:], x[P : 2 * P, :])
@@ -123,13 +127,23 @@ def tile_lcnspiking_b_kernel(tc, x, w0, b0, w1, b1, w2, b2, w3, b3, w4, b4, fc_w
         load_blocks(nc, w3_tile, w3, 0, D3 // P)
         load_blocks(nc, w4_tile, w4, 0, D4 // P)
         load_blocks(nc, fcw_tile, fc_w, 0, D5 // P)
-        fcb_rows = held.tile([P, OUT], F32, name="fcb_rows")
-        nc.sync.dma_start(fcb_rows[:], fc_b.rearrange("e o -> o e").broadcast_to([P, OUT]))
         nc.sync.dma_start(x_blocks[2][:], x[2 * P : 3 * P, :])
 
         identity = held.tile([P, P], F32, name="identity")
         make_identity(nc, identity[:])
-        b0_tile, b1_tile, b2_tile, b3_tile, b4_tile = load_biases(nc, held, flipped, identity, [b0, b1, b2, b3, b4])
+
+        bias_columns = turn_rows(nc, held, flipped, identity, "bias_columns", bias_rows)
+        w0_columns = turn_rows(nc, held, flipped, identity, "w0_columns", w0_rows)
+        for c in range(CHUNKS):
+            for k in range(KN):
+                spread(nc, flipped, identity, w0_columns, (k * D1 + c * CHUNK) // P, w0_chunks[c][:, k, :])
+
+        first_column = [sum(b.shape[0] // P for b in biases[:i]) for i in range(len(biases))]
+        b0_tile, b1_tile, b2_tile, b3_tile, b4_tile = [
+            bias_columns[:, first : first + b.shape[0] // P] for first, b in zip(first_column[:-1], biases[:-1])
+        ]
+        fcb_rows = held.tile([P, OUT], F32, name="fcb_rows")
+        spread(nc, flipped, identity, bias_columns, first_column[-1], fcb_rows[:])
 
         for b in range(SAMPLE_BLOCKS):
             y0 = acts.tile([P, D1 // P, P], BF16, name="y0")
@@ -144,7 +158,7 @@ def tile_lcnspiking_b_kernel(tc, x, w0, b0, w1, b1, w2, b2, w3, b3, w4, b4, fc_w
                         w0_chunks[c][:, k, :],
                         MULT,
                     )
-                y0_sum = flipped.tile([P, CHUNK // P, P], F32, name="y0_sum")
+                y0_sum = flipped.tile([P, CHUNK // P, P], F32, name="y0_sum", tag="bank")
                 for k in range(KN):
                     for i in range(CHUNK // P):
                         nc.tensor.matmul(

@@ -104,7 +104,7 @@ def tile_lcnspiking_b_kernel(tc, x, w0, b0, w1, b1, w2, b2, w3, b3, w4, b4, fc_w
         offsets = held.tile([P, N // 16], U16, name="offsets")
         nc.sync.dma_start(offsets[:], offs)
 
-        w0_chunks = [held.tile([P, KN, CHUNK], F32, name="w0_chunk%d" % c) for c in range(CHUNKS)]
+        w0_spread = held.tile([P, KN, D1], F32, name="w0_spread")
         x_blocks = [held.tile([P, S], F32, name="x_block%d" % b) for b in range(SAMPLE_BLOCKS)]
 
         w1_tile = weight_tile(held, "w1_tile", w1)
@@ -132,12 +132,12 @@ def tile_lcnspiking_b_kernel(tc, x, w0, b0, w1, b1, w2, b2, w3, b3, w4, b4, fc_w
         identity = held.tile([P, P], F32, name="identity")
         make_identity(nc, identity[:])
 
-        bias_columns = turn_rows(nc, held, flipped, identity, "bias_columns", bias_rows)
         w0_columns = turn_rows(nc, held, flipped, identity, "w0_columns", w0_rows)
         for c in range(CHUNKS):
             for k in range(KN):
-                spread(nc, flipped, identity, w0_columns, (k * D1 + c * CHUNK) // P, w0_chunks[c][:, k, :])
+                spread(nc, flipped, identity, w0_columns, (k * D1 + c * CHUNK) // P, w0_spread[:, k, c * CHUNK : (c + 1) * CHUNK])
 
+        bias_columns = turn_rows(nc, held, flipped, identity, "bias_columns", bias_rows)
         first_column = [sum(b.shape[0] // P for b in biases[:i]) for i in range(len(biases))]
         b0_tile, b1_tile, b2_tile, b3_tile, b4_tile = [
             bias_columns[:, first : first + b.shape[0] // P] for first, b in zip(first_column[:-1], biases[:-1])
@@ -148,32 +148,39 @@ def tile_lcnspiking_b_kernel(tc, x, w0, b0, w1, b1, w2, b2, w3, b3, w4, b4, fc_w
         for b in range(SAMPLE_BLOCKS):
             y0 = acts.tile([P, D1 // P, P], BF16, name="y0")
             h1_banks = open_banks(sums, w1_tile)
-            for c in range(CHUNKS):
+            widths = [CHUNK] * CHUNKS
+            if b == SAMPLE_BLOCKS - 1:
+                widths = [CHUNK] * (CHUNKS - 1) + [P] * (CHUNK // P)
+            first_node = 0
+            for width in widths:
+                blocks = width // P
+                first_block = first_node // P
                 prod = products.tile([P, KN, CHUNK], F32, name="prod")
                 for k in range(KN):
-                    first = (k * D1 + c * CHUNK) // 16
+                    first = (k * D1 + first_node) // 16
                     nc.vector.tensor_tensor(
-                        prod[:, k, :],
-                        x_blocks[b][:].indirect(offsets[:, first : first + CHUNK // 16]),
-                        w0_chunks[c][:, k, :],
+                        prod[:, k, 0:width],
+                        x_blocks[b][:].indirect(offsets[:, first : first + width // 16]),
+                        w0_spread[:, k, first_node : first_node + width],
                         MULT,
                     )
                 y0_sum = flipped.tile([P, CHUNK // P, P], F32, name="y0_sum", tag="bank")
                 for k in range(KN):
-                    for i in range(CHUNK // P):
+                    for i in range(blocks):
                         nc.tensor.matmul(
                             y0_sum[:, i, :],
                             lhsT=prod[:, k, i * P : (i + 1) * P],
                             rhs=identity[:],
                             is_transpose=True,
                             start=(k == 0 and i == 0),
-                            stop=(k == KN - 1 and i == CHUNK // P - 1),
+                            stop=(k == KN - 1 and i == blocks - 1),
                         )
-                for i in range(CHUNK // P):
-                    j = c * (CHUNK // P) + i
+                for i in range(blocks):
+                    j = first_block + i
                     nc.scalar.activation(y0[:, j, :], y0_sum[:, i, :], IDENTITY, bias=b0_tile[:, j : j + 1])
-                for i in range(CHUNK // P):
-                    add_block(nc, h1_banks, w1_tile, y0, c * (CHUNK // P) + i)
+                for i in range(blocks):
+                    add_block(nc, h1_banks, w1_tile, y0, first_block + i)
+                first_node += width
 
             h1 = add_bias(nc, acts, "h1", h1_banks, b1_tile)
             h2 = dense_layer(nc, sums, acts, "h2", w2_tile, b2_tile, h1)

@@ -13,8 +13,9 @@ C, S, KN = 384, 4096, 4
 D1, D2, D3, D4, D5, OUT = 2048, 1024, 512, 256, 128, 128
 N = KN * D1
 SAMPLE_BLOCKS = C // P
-CHUNK = 512
-CHUNKS = D1 // CHUNK
+BANK = 512
+PIECE = 512
+STEP = PIECE // KN
 BANK_BLOCKS = 4
 
 FLOPS = 2 * C * (N + D1 * D2 + D2 * D3 + D3 * D4 + D4 * D5 + D5 * OUT)
@@ -38,7 +39,7 @@ def load_bias_rows(nc, rows, biases):
 
 def turn_rows(nc, held, flipped, identity, name, rows):
     count = rows.shape[0]
-    turned = flipped.tile([P, CHUNK], F32, name="turned", tag="bank")
+    turned = flipped.tile([P, BANK], F32, name="turned", tag="bank")
     nc.tensor.transpose(turned[:, 0:count], rows[:], identity[0:count, 0:count])
     columns = held.tile([P, count], F32, name=name)
     nc.scalar.activation(columns[:], turned[:, 0:count], IDENTITY)
@@ -47,7 +48,7 @@ def turn_rows(nc, held, flipped, identity, name, rows):
 
 def spread(nc, flipped, identity, columns, first, out_rows):
     width = out_rows.shape[1]
-    repeated = flipped.tile([P, CHUNK], F32, name="repeated", tag="bank")
+    repeated = flipped.tile([P, BANK], F32, name="repeated", tag="bank")
     for i in range(width // P):
         column = columns[:, first + i : first + i + 1]
         nc.tensor.transpose(repeated[:, i * P : (i + 1) * P], column.to_broadcast([P, P]), identity[:])
@@ -94,7 +95,7 @@ def tile_lcnspiking_b_kernel(tc, x, w0, b0, w1, b1, w2, b2, w3, b3, w4, b4, fc_w
     nc = tc.nc
     with (
         tc.tile_pool(name="held", bufs=1) as held,
-        tc.tile_pool(name="products", bufs=4) as products,
+        tc.tile_pool(name="products", bufs=2) as products,
         tc.tile_pool(name="acts", bufs=2) as acts,
         tc.psum_pool(name="flipped", bufs=3) as flipped,
         tc.psum_pool(name="sums", bufs=5) as sums,
@@ -133,9 +134,9 @@ def tile_lcnspiking_b_kernel(tc, x, w0, b0, w1, b1, w2, b2, w3, b3, w4, b4, fc_w
         make_identity(nc, identity[:])
 
         w0_columns = turn_rows(nc, held, flipped, identity, "w0_columns", w0_rows)
-        for c in range(CHUNKS):
+        for d in range(0, D1, BANK):
             for k in range(KN):
-                spread(nc, flipped, identity, w0_columns, (k * D1 + c * CHUNK) // P, w0_spread[:, k, c * CHUNK : (c + 1) * CHUNK])
+                spread(nc, flipped, identity, w0_columns, (k * D1 + d) // P, w0_spread[:, k, d : d + BANK])
 
         bias_columns = turn_rows(nc, held, flipped, identity, "bias_columns", bias_rows)
         first_column = [sum(b.shape[0] // P for b in biases[:i]) for i in range(len(biases))]
@@ -148,39 +149,34 @@ def tile_lcnspiking_b_kernel(tc, x, w0, b0, w1, b1, w2, b2, w3, b3, w4, b4, fc_w
         for b in range(SAMPLE_BLOCKS):
             y0 = acts.tile([P, D1 // P, P], BF16, name="y0")
             h1_banks = open_banks(sums, w1_tile)
-            widths = [CHUNK] * CHUNKS
-            if b == SAMPLE_BLOCKS - 1:
-                widths = [CHUNK] * (CHUNKS - 1) + [P] * (CHUNK // P)
-            first_node = 0
-            for width in widths:
-                blocks = width // P
-                first_block = first_node // P
-                prod = products.tile([P, KN, CHUNK], F32, name="prod")
-                for k in range(KN):
-                    first = (k * D1 + first_node) // 16
-                    nc.vector.tensor_tensor(
-                        prod[:, k, 0:width],
-                        x_blocks[b][:].indirect(offsets[:, first : first + width // 16]),
-                        w0_spread[:, k, first_node : first_node + width],
-                        MULT,
-                    )
-                y0_sum = flipped.tile([P, CHUNK // P, P], F32, name="y0_sum", tag="bank")
-                for k in range(KN):
-                    for i in range(blocks):
-                        nc.tensor.matmul(
-                            y0_sum[:, i, :],
-                            lhsT=prod[:, k, i * P : (i + 1) * P],
-                            rhs=identity[:],
-                            is_transpose=True,
-                            start=(k == 0 and i == 0),
-                            stop=(k == KN - 1 and i == blocks - 1),
-                        )
-                for i in range(blocks):
-                    j = first_block + i
-                    nc.scalar.activation(y0[:, j, :], y0_sum[:, i, :], IDENTITY, bias=b0_tile[:, j : j + 1])
-                for i in range(blocks):
-                    add_block(nc, h1_banks, w1_tile, y0, first_block + i)
-                first_node += width
+            prod = products.tile([P, KN, D1], F32, name="prod")
+            for r in range(D1 // STEP + KN - 1):
+                k = r % KN
+                begin = (r - (KN - 1)) * STEP
+                first, last = max(begin, 0), min(begin + PIECE, D1)
+                nc.vector.tensor_tensor(
+                    prod[:, k, first:last],
+                    x_blocks[b][:].indirect(offsets[:, (k * D1 + first) // 16 : (k * D1 + last) // 16]),
+                    w0_spread[:, k, first:last],
+                    MULT,
+                )
+                if begin >= 0:
+                    y0_sum = flipped.tile([P, BANK_BLOCKS, P], F32, name="y0_sum", tag="bank")
+                    for turn in range(1, KN + 1):
+                        for i in range(STEP // P):
+                            nc.tensor.matmul(
+                                y0_sum[:, i, :],
+                                lhsT=prod[:, (k + turn) % KN, begin + i * P : begin + (i + 1) * P],
+                                rhs=identity[:],
+                                is_transpose=True,
+                                start=(turn == 1 and i == 0),
+                                stop=(turn == KN and i == STEP // P - 1),
+                            )
+                    for i in range(STEP // P):
+                        j = begin // P + i
+                        nc.scalar.activation(y0[:, j, :], y0_sum[:, i, :], IDENTITY, bias=b0_tile[:, j : j + 1])
+                    for i in range(STEP // P):
+                        add_block(nc, h1_banks, w1_tile, y0, begin // P + i)
 
             h1 = add_bias(nc, acts, "h1", h1_banks, b1_tile)
             h2 = dense_layer(nc, sums, acts, "h2", w2_tile, b2_tile, h1)

@@ -5,7 +5,6 @@ F32 = mybir.dt.float32
 BF16 = mybir.dt.bfloat16
 U16 = mybir.dt.uint16
 MULT = mybir.AluOpType.mult
-ADD = mybir.AluOpType.add
 IDENTITY = mybir.ActivationFunctionType.Identity
 
 P = 128
@@ -16,6 +15,7 @@ SAMPLE_BLOCKS = C // P
 BANK = 512
 PIECE = 512
 STEP = PIECE // KN
+LAG = 2
 BANK_BLOCKS = 4
 
 FLOPS = 2 * C * (N + D1 * D2 + D2 * D3 + D3 * D4 + D4 * D5 + D5 * OUT)
@@ -143,9 +143,31 @@ def tile_lcnspiking_b_kernel(tc, x, w0, b0, w1, b1, w2, b2, w3, b3, w4, b4, fc_w
         b0_tile, b1_tile, b2_tile, b3_tile, b4_tile = [
             bias_columns[:, first : first + b.shape[0] // P] for first, b in zip(first_column[:-1], biases[:-1])
         ]
-        fcb_rows = held.tile([P, OUT], F32, name="fcb_rows")
-        spread(nc, flipped, identity, bias_columns, first_column[-1], fcb_rows[:])
+        fcb_column = bias_columns[:, first_column[-1] : first_column[-1] + 1]
 
+        def finish_block(b, h1_banks):
+            h1 = add_bias(nc, acts, "h1", h1_banks, b1_tile)
+            h2 = dense_layer(nc, sums, acts, "h2", w2_tile, b2_tile, h1)
+            h3 = dense_layer(nc, sums, acts, "h3", w3_tile, b3_tile, h2)
+            h4 = dense_layer(nc, sums, acts, "h4", w4_tile, b4_tile, h3)
+            out_sum = sums.tile([P, BANK_BLOCKS, P], F32, name="acc")
+            nc.tensor.matmul(
+                out_sum[:, 0, :], lhsT=fcb_column.to_broadcast([P, P]), rhs=identity[:], is_transpose=True, start=True, stop=False
+            )
+            nc.tensor.matmul(out_sum[:, 0, :], lhsT=h4[:, 0, :], rhs=fcw_tile[:, 0, :], start=False, stop=True)
+            out_rows = acts.tile([P, OUT], F32, name="out_rows")
+            nc.scalar.activation(out_rows[:], out_sum[:, 0, :], IDENTITY)
+            nc.sync.dma_start(out[b * P : (b + 1) * P, :], out_rows[:])
+
+        def second_layer(rounded):
+            due, b, begin, y0, h1_banks = rounded
+            for i in range(STEP // P):
+                add_block(nc, h1_banks, w1_tile, y0, begin // P + i)
+            if begin + STEP == D1:
+                finish_block(b, h1_banks)
+
+        waiting = []
+        gathers = 0
         for b in range(SAMPLE_BLOCKS):
             y0 = acts.tile([P, D1 // P, P], BF16, name="y0")
             h1_banks = open_banks(sums, w1_tile)
@@ -172,19 +194,14 @@ def tile_lcnspiking_b_kernel(tc, x, w0, b0, w1, b1, w2, b2, w3, b3, w4, b4, fc_w
                                 start=(turn == 1 and i == 0),
                                 stop=(turn == KN and i == STEP // P - 1),
                             )
+                gathers += 1
+                if waiting and waiting[0][0] <= gathers:
+                    second_layer(waiting[0])
+                    waiting = waiting[1:]
+                if begin >= 0:
                     for i in range(STEP // P):
                         j = begin // P + i
                         nc.scalar.activation(y0[:, j, :], y0_sum[:, i, :], IDENTITY, bias=b0_tile[:, j : j + 1])
-                    for i in range(STEP // P):
-                        add_block(nc, h1_banks, w1_tile, y0, begin // P + i)
-
-            h1 = add_bias(nc, acts, "h1", h1_banks, b1_tile)
-            h2 = dense_layer(nc, sums, acts, "h2", w2_tile, b2_tile, h1)
-            h3 = dense_layer(nc, sums, acts, "h3", w3_tile, b3_tile, h2)
-            h4 = dense_layer(nc, sums, acts, "h4", w4_tile, b4_tile, h3)
-
-            out_sum = sums.tile([P, BANK_BLOCKS, P], F32, name="acc")
-            nc.tensor.matmul(out_sum[:, 0, :], lhsT=h4[:, 0, :], rhs=fcw_tile[:, 0, :], start=True, stop=True)
-            out_rows = acts.tile([P, OUT], F32, name="out_rows")
-            nc.vector.tensor_tensor(out_rows[:], out_sum[:, 0, :], fcb_rows[:], ADD)
-            nc.sync.dma_start(out[b * P : (b + 1) * P, :], out_rows[:])
+                    waiting.append((gathers + LAG, b, begin, y0, h1_banks))
+        for rounded in waiting:
+            second_layer(rounded)

@@ -95,7 +95,6 @@ def tile_lcnspiking_b_kernel(tc, x, w0, b0, w1, b1, w2, b2, w3, b3, w4, b4, fc_w
     nc = tc.nc
     with (
         tc.tile_pool(name="held", bufs=1) as held,
-        tc.tile_pool(name="products", bufs=2) as products,
         tc.tile_pool(name="acts", bufs=2) as acts,
         tc.psum_pool(name="flipped", bufs=3) as flipped,
         tc.psum_pool(name="sums", bufs=5) as sums,
@@ -168,10 +167,10 @@ def tile_lcnspiking_b_kernel(tc, x, w0, b0, w1, b1, w2, b2, w3, b3, w4, b4, fc_w
 
         waiting = []
         gathers = 0
+        prod = held.tile([P, KN, D1], F32, name="prod")
         for b in range(SAMPLE_BLOCKS):
             y0 = acts.tile([P, D1 // P, P], BF16, name="y0")
             h1_banks = open_banks(sums, w1_tile)
-            prod = products.tile([P, KN, D1], F32, name="prod")
             for r in range(D1 // STEP + KN - 1):
                 k = r % KN
                 begin = (r - (KN - 1)) * STEP

@@ -16,9 +16,26 @@ BANK = 512
 PIECE = 512
 STEP = PIECE // KN
 LAG = 2
+PLAIN_END = 256
 BANK_BLOCKS = 4
 
 FLOPS = 2 * C * (N + D1 * D2 + D2 * D3 + D3 * D4 + D4 * D5 + D5 * OUT)
+
+
+def staggered_cuts(low, high):
+    cuts = []
+    for r in range((high - low) // STEP + KN - 1):
+        begin = low + (r - (KN - 1)) * STEP
+        cuts.append((r % KN, max(begin, low), min(begin + PIECE, high), begin if begin >= low else None, True))
+    return cuts
+
+
+def plain_cuts(low, high):
+    cuts = []
+    for begin in range(low, high, STEP):
+        for k in range(KN):
+            cuts.append((k, begin, begin + STEP, begin if k == KN - 1 else None, k == KN - 1))
+    return cuts
 
 
 def weight_tile(pool, name, w):
@@ -55,18 +72,20 @@ def spread(nc, flipped, identity, columns, first, out_rows):
     nc.scalar.activation(out_rows, repeated[:, 0:width], IDENTITY)
 
 
-def open_banks(sums, w_tile):
+def open_banks(sums, w_tile, samples):
     blocks_out = w_tile.shape[2] // P
-    return [sums.tile([P, BANK_BLOCKS, P], F32, name="acc") for m0 in range(0, blocks_out, BANK_BLOCKS)]
+    bank_blocks = BANK // samples
+    return [sums.tile([P, bank_blocks, samples], F32, name="acc") for m0 in range(0, blocks_out, bank_blocks)]
 
 
 def add_block(nc, banks, w_tile, h_in, j):
     blocks_in, blocks_out = w_tile.shape[1], w_tile.shape[2] // P
+    bank_blocks = banks[0].shape[1]
     for m in range(blocks_out):
-        place = m % BANK_BLOCKS
-        last_of_bank = place == BANK_BLOCKS - 1 or m == blocks_out - 1
+        place = m % bank_blocks
+        last_of_bank = place == bank_blocks - 1 or m == blocks_out - 1
         nc.tensor.matmul(
-            banks[m // BANK_BLOCKS][:, place, :],
+            banks[m // bank_blocks][:, place, :],
             lhsT=w_tile[:, j, m * P : (m + 1) * P],
             rhs=h_in[:, j, :],
             start=(j == 0 and place == 0),
@@ -74,21 +93,21 @@ def add_block(nc, banks, w_tile, h_in, j):
         )
 
 
-def add_bias(nc, acts, name, banks, b_tile):
-    blocks_out = b_tile.shape[1]
-    h_out = acts.tile([P, blocks_out, P], BF16, name=name)
-    for m in range(blocks_out):
-        nc.scalar.activation(
-            h_out[:, m, :], banks[m // BANK_BLOCKS][:, m % BANK_BLOCKS, :], IDENTITY, bias=b_tile[:, m : m + 1]
-        )
-    return h_out
+def add_bias(nc, h_out, banks, b_tile, on_vector):
+    bank_blocks = banks[0].shape[1]
+    for m in range(b_tile.shape[1]):
+        block_sum = banks[m // bank_blocks][:, m % bank_blocks, :]
+        if on_vector:
+            nc.vector.tensor_scalar_add(h_out[:, m, :], block_sum, b_tile[:, m : m + 1])
+        else:
+            nc.scalar.activation(h_out[:, m, :], block_sum, IDENTITY, bias=b_tile[:, m : m + 1])
 
 
-def dense_layer(nc, sums, acts, name, w_tile, b_tile, h_in):
-    banks = open_banks(sums, w_tile)
+def dense_layer(nc, sums, w_tile, b_tile, h_in, h_out, on_vector):
+    banks = open_banks(sums, w_tile, h_in.shape[2])
     for j in range(w_tile.shape[1]):
         add_block(nc, banks, w_tile, h_in, j)
-    return add_bias(nc, acts, name, banks, b_tile)
+    add_bias(nc, h_out, banks, b_tile, on_vector)
 
 
 def tile_lcnspiking_b_kernel(tc, x, w0, b0, w1, b1, w2, b2, w3, b3, w4, b4, fc_w, fc_b, offs, out):
@@ -144,44 +163,66 @@ def tile_lcnspiking_b_kernel(tc, x, w0, b0, w1, b1, w2, b2, w3, b3, w4, b4, fc_w
         ]
         fcb_column = bias_columns[:, first_column[-1] : first_column[-1] + 1]
 
-        def finish_block(b, h1_banks):
-            h1 = add_bias(nc, acts, "h1", h1_banks, b1_tile)
-            h2 = dense_layer(nc, sums, acts, "h2", w2_tile, b2_tile, h1)
-            h3 = dense_layer(nc, sums, acts, "h3", w3_tile, b3_tile, h2)
-            h4 = dense_layer(nc, sums, acts, "h4", w4_tile, b4_tile, h3)
+        h2_blocks = [held.tile([P, D3 // P, P], BF16, name="h2_block%d" % b) for b in range(SAMPLE_BLOCKS)]
+        h3_blocks = [held.tile([P, D4 // P, P], BF16, name="h3_block%d" % b) for b in range(SAMPLE_BLOCKS)]
+        h4_blocks = [held.tile([P, D5 // P, P], BF16, name="h4_block%d" % b) for b in range(SAMPLE_BLOCKS)]
+
+        def third_layer(h1_banks, h2):
+            h1 = acts.tile([P, D2 // P, P], BF16, name="h1")
+            add_bias(nc, h1, h1_banks, b1_tile, False)
+            dense_layer(nc, sums, w2_tile, b2_tile, h1, h2, False)
+
+        def read_out(b, h4, on_vector):
             out_sum = sums.tile([P, BANK_BLOCKS, P], F32, name="acc")
             nc.tensor.matmul(
                 out_sum[:, 0, :], lhsT=fcb_column.to_broadcast([P, P]), rhs=identity[:], is_transpose=True, start=True, stop=False
             )
-            nc.tensor.matmul(out_sum[:, 0, :], lhsT=h4[:, 0, :], rhs=fcw_tile[:, 0, :], start=False, stop=True)
-            out_rows = acts.tile([P, OUT], F32, name="out_rows")
-            nc.scalar.activation(out_rows[:], out_sum[:, 0, :], IDENTITY)
+            nc.tensor.matmul(out_sum[:, 0, :], lhsT=h4, rhs=fcw_tile[:, 0, :], start=False, stop=True)
+            out_rows = held.tile([P, OUT], F32, name="out_rows%d" % b)
+            if on_vector:
+                nc.vector.tensor_copy(out_rows[:], out_sum[:, 0, :])
+            else:
+                nc.scalar.activation(out_rows[:], out_sum[:, 0, :], IDENTITY)
             nc.sync.dma_start(out[b * P : (b + 1) * P, :], out_rows[:])
 
         def second_layer(rounded):
             due, b, begin, y0, h1_banks = rounded
             for i in range(STEP // P):
                 add_block(nc, h1_banks, w1_tile, y0, begin // P + i)
-            if begin + STEP == D1:
-                finish_block(b, h1_banks)
+            if begin + STEP < D1:
+                return
+            before = b - 1
+            if b == SAMPLE_BLOCKS - 1:
+                dense_layer(nc, sums, w3_tile, b3_tile, h2_blocks[before], h3_blocks[before], True)
+            third_layer(h1_banks, h2_blocks[b])
+            if b == SAMPLE_BLOCKS - 2:
+                return
+            if b == SAMPLE_BLOCKS - 1:
+                dense_layer(nc, sums, w4_tile, b4_tile, h3_blocks[before], h4_blocks[before], True)
+            dense_layer(nc, sums, w3_tile, b3_tile, h2_blocks[b], h3_blocks[b], False)
+            if b == SAMPLE_BLOCKS - 1:
+                read_out(before, h4_blocks[before][:, 0, :], True)
+            dense_layer(nc, sums, w4_tile, b4_tile, h3_blocks[b], h4_blocks[b], False)
+            read_out(b, h4_blocks[b][:, 0, :], False)
 
         waiting = []
-        gathers = 0
+        steps = 0
         prod = held.tile([P, KN, D1], F32, name="prod")
         for b in range(SAMPLE_BLOCKS):
             y0 = acts.tile([P, D1 // P, P], BF16, name="y0")
-            h1_banks = open_banks(sums, w1_tile)
-            for r in range(D1 // STEP + KN - 1):
-                k = r % KN
-                begin = (r - (KN - 1)) * STEP
-                first, last = max(begin, 0), min(begin + PIECE, D1)
+            h1_banks = open_banks(sums, w1_tile, P)
+            if b == SAMPLE_BLOCKS - 1:
+                cuts = staggered_cuts(0, D1 - PLAIN_END) + plain_cuts(D1 - PLAIN_END, D1)
+            else:
+                cuts = staggered_cuts(0, D1)
+            for k, first, last, begin, step_ends in cuts:
                 nc.vector.tensor_tensor(
                     prod[:, k, first:last],
                     x_blocks[b][:].indirect(offsets[:, (k * D1 + first) // 16 : (k * D1 + last) // 16]),
                     w0_spread[:, k, first:last],
                     MULT,
                 )
-                if begin >= 0:
+                if begin is not None:
                     y0_sum = flipped.tile([P, BANK_BLOCKS, P], F32, name="y0_sum", tag="bank")
                     for turn in range(1, KN + 1):
                         for i in range(STEP // P):
@@ -193,14 +234,15 @@ def tile_lcnspiking_b_kernel(tc, x, w0, b0, w1, b1, w2, b2, w3, b3, w4, b4, fc_w
                                 start=(turn == 1 and i == 0),
                                 stop=(turn == KN and i == STEP // P - 1),
                             )
-                gathers += 1
-                if waiting and waiting[0][0] <= gathers:
-                    second_layer(waiting[0])
-                    waiting = waiting[1:]
-                if begin >= 0:
+                if step_ends:
+                    steps += 1
+                    if waiting and waiting[0][0] <= steps:
+                        second_layer(waiting[0])
+                        waiting = waiting[1:]
+                if begin is not None:
                     for i in range(STEP // P):
                         j = begin // P + i
                         nc.scalar.activation(y0[:, j, :], y0_sum[:, i, :], IDENTITY, bias=b0_tile[:, j : j + 1])
-                    waiting.append((gathers + LAG, b, begin, y0, h1_banks))
+                    waiting.append((steps + LAG, b, begin, y0, h1_banks))
         for rounded in waiting:
             second_layer(rounded)

@@ -15,7 +15,7 @@ SAMPLE_BLOCKS = C // P
 BANK = 512
 PIECE = 512
 STEP = PIECE // KN
-LAG = 2
+LAG = 1
 PLAIN_END = 256
 BANK_BLOCKS = 4
 

@@ -167,10 +167,10 @@ def tile_lcnspiking_b_kernel(tc, x, w0, b0, w1, b1, w2, b2, w3, b3, w4, b4, fc_w
         h3_blocks = [held.tile([P, D4 // P, P], BF16, name="h3_block%d" % b) for b in range(SAMPLE_BLOCKS)]
         h4_blocks = [held.tile([P, D5 // P, P], BF16, name="h4_block%d" % b) for b in range(SAMPLE_BLOCKS)]
 
-        def third_layer(h1_banks, h2):
+        def third_layer(h1_banks, h2, on_vector):
             h1 = acts.tile([P, D2 // P, P], BF16, name="h1")
-            add_bias(nc, h1, h1_banks, b1_tile, False)
-            dense_layer(nc, sums, w2_tile, b2_tile, h1, h2, False)
+            add_bias(nc, h1, h1_banks, b1_tile, on_vector)
+            dense_layer(nc, sums, w2_tile, b2_tile, h1, h2, on_vector)
 
         def read_out(b, h4, on_vector):
             out_sum = sums.tile([P, BANK_BLOCKS, P], F32, name="acc")
@@ -192,18 +192,19 @@ def tile_lcnspiking_b_kernel(tc, x, w0, b0, w1, b1, w2, b2, w3, b3, w4, b4, fc_w
             if begin + STEP < D1:
                 return
             before = b - 1
-            if b == SAMPLE_BLOCKS - 1:
-                dense_layer(nc, sums, w3_tile, b3_tile, h2_blocks[before], h3_blocks[before], True)
-            third_layer(h1_banks, h2_blocks[b])
+            is_last = b == SAMPLE_BLOCKS - 1
+            if is_last:
+                dense_layer(nc, sums, w3_tile, b3_tile, h2_blocks[before], h3_blocks[before], False)
+            third_layer(h1_banks, h2_blocks[b], is_last)
             if b == SAMPLE_BLOCKS - 2:
                 return
-            if b == SAMPLE_BLOCKS - 1:
-                dense_layer(nc, sums, w4_tile, b4_tile, h3_blocks[before], h4_blocks[before], True)
-            dense_layer(nc, sums, w3_tile, b3_tile, h2_blocks[b], h3_blocks[b], False)
-            if b == SAMPLE_BLOCKS - 1:
-                read_out(before, h4_blocks[before][:, 0, :], True)
-            dense_layer(nc, sums, w4_tile, b4_tile, h3_blocks[b], h4_blocks[b], False)
-            read_out(b, h4_blocks[b][:, 0, :], False)
+            if is_last:
+                dense_layer(nc, sums, w4_tile, b4_tile, h3_blocks[before], h4_blocks[before], False)
+            dense_layer(nc, sums, w3_tile, b3_tile, h2_blocks[b], h3_blocks[b], is_last)
+            if is_last:
+                read_out(before, h4_blocks[before][:, 0, :], False)
+            dense_layer(nc, sums, w4_tile, b4_tile, h3_blocks[b], h4_blocks[b], is_last)
+            read_out(b, h4_blocks[b][:, 0, :], is_last)
 
         waiting = []
         steps = 0
@@ -240,9 +241,13 @@ def tile_lcnspiking_b_kernel(tc, x, w0, b0, w1, b1, w2, b2, w3, b3, w4, b4, fc_w
                         second_layer(waiting[0])
                         waiting = waiting[1:]
                 if begin is not None:
+                    very_last = b == SAMPLE_BLOCKS - 1 and begin + STEP == D1
                     for i in range(STEP // P):
                         j = begin // P + i
-                        nc.scalar.activation(y0[:, j, :], y0_sum[:, i, :], IDENTITY, bias=b0_tile[:, j : j + 1])
+                        if very_last:
+                            nc.vector.tensor_scalar_add(y0[:, j, :], y0_sum[:, i, :], b0_tile[:, j : j + 1])
+                        else:
+                            nc.scalar.activation(y0[:, j, :], y0_sum[:, i, :], IDENTITY, bias=b0_tile[:, j : j + 1])
                     waiting.append((steps + LAG, b, begin, y0, h1_banks))
         for rounded in waiting:
             second_layer(rounded)

@@ -191,18 +191,9 @@ def tile_lcnspiking_b_kernel(tc, x, w0, b0, w1, b1, w2, b2, w3, b3, w4, b4, fc_w
                 add_block(nc, h1_banks, w1_tile, y0, begin // P + i)
             if begin + STEP < D1:
                 return
-            before = b - 1
             is_last = b == SAMPLE_BLOCKS - 1
-            if is_last:
-                dense_layer(nc, sums, w3_tile, b3_tile, h2_blocks[before], h3_blocks[before], False)
             third_layer(h1_banks, h2_blocks[b], is_last)
-            if b == SAMPLE_BLOCKS - 2:
-                return
-            if is_last:
-                dense_layer(nc, sums, w4_tile, b4_tile, h3_blocks[before], h4_blocks[before], False)
             dense_layer(nc, sums, w3_tile, b3_tile, h2_blocks[b], h3_blocks[b], is_last)
-            if is_last:
-                read_out(before, h4_blocks[before][:, 0, :], False)
             dense_layer(nc, sums, w4_tile, b4_tile, h3_blocks[b], h4_blocks[b], is_last)
             read_out(b, h4_blocks[b][:, 0, :], is_last)
 

import concourse.mybir as mybir
from concourse.masks import make_identity

F32 = mybir.dt.float32
BF16 = mybir.dt.bfloat16
U16 = mybir.dt.uint16
MULT = mybir.AluOpType.mult
IDENTITY = mybir.ActivationFunctionType.Identity

P = 128
C, S, KN = 384, 4096, 4
D1, D2, D3, D4, D5, OUT = 2048, 1024, 512, 256, 128, 128
N = KN * D1
SAMPLE_BLOCKS = C // P
BANK = 512
PIECE = 512
STEP = PIECE // KN
LAG = 1
PLAIN_END = 256
BANK_BLOCKS = 4

FLOPS = 2 * C * (N + D1 * D2 + D2 * D3 + D3 * D4 + D4 * D5 + D5 * OUT)


def staggered_cuts(low, high):
    cuts = []
    for r in range((high - low) // STEP + KN - 1):
        begin = low + (r - (KN - 1)) * STEP
        cuts.append((r % KN, max(begin, low), min(begin + PIECE, high), begin if begin >= low else None, True))
    return cuts


def plain_cuts(low, high):
    cuts = []
    for begin in range(low, high, STEP):
        for k in range(KN):
            cuts.append((k, begin, begin + STEP, begin if k == KN - 1 else None, k == KN - 1))
    return cuts


def weight_tile(pool, name, w):
    return pool.tile([P, w.shape[0] // P, w.shape[1]], BF16, name=name)


def load_blocks(nc, w_tile, w, j0, j1):
    nc.sync.dma_start(w_tile[:, j0:j1, :], w.rearrange("(j p) e -> p j e", p=P)[:, j0:j1, :])


def load_bias_rows(nc, rows, biases):
    used = 0
    for b in biases:
        blocks = b.shape[0] // P
        nc.sync.dma_start(rows[used : used + blocks, :], b.rearrange("(j p) o -> j (p o)", p=P))
        used += blocks


def turn_rows(nc, held, flipped, identity, name, rows):
    count = rows.shape[0]
    turned = flipped.tile([P, BANK], F32, name="turned", tag="bank")
    nc.tensor.transpose(turned[:, 0:count], rows[:], identity[0:count, 0:count])
    columns = held.tile([P, count], F32, name=name)
    nc.scalar.activation(columns[:], turned[:, 0:count], IDENTITY)
    return columns


def spread(nc, flipped, identity, columns, first, out_rows):
    width = out_rows.shape[1]
    repeated = flipped.tile([P, BANK], F32, name="repeated", tag="bank")
    for i in range(width // P):
        column = columns[:, first + i : first + i + 1]
        nc.tensor.transpose(repeated[:, i * P : (i + 1) * P], column.to_broadcast([P, P]), identity[:])
    nc.scalar.activation(out_rows, repeated[:, 0:width], IDENTITY)


def open_banks(sums, w_tile, samples):
    blocks_out = w_tile.shape[2] // P
    bank_blocks = BANK // samples
    return [sums.tile([P, bank_blocks, samples], F32, name="acc") for m0 in range(0, blocks_out, bank_blocks)]


def add_block(nc, banks, w_tile, h_in, j):
    blocks_in, blocks_out = w_tile.shape[1], w_tile.shape[2] // P
    bank_blocks = banks[0].shape[1]
    for m in range(blocks_out):
        place = m % bank_blocks
        last_of_bank = place == bank_blocks - 1 or m == blocks_out - 1
        nc.tensor.matmul(
            banks[m // bank_blocks][:, place, :],
            lhsT=w_tile[:, j, m * P : (m + 1) * P],
            rhs=h_in[:, j, :],
            start=(j == 0 and place == 0),
            stop=(j == blocks_in - 1 and last_of_bank),
        )


def add_bias(nc, h_out, banks, b_tile, on_vector):
    bank_blocks = banks[0].shape[1]
    for m in range(b_tile.shape[1]):
        block_sum = banks[m // bank_blocks][:, m % bank_blocks, :]
        if on_vector:
            nc.vector.tensor_scalar_add(h_out[:, m, :], block_sum, b_tile[:, m : m + 1])
        else:
            nc.scalar.activation(h_out[:, m, :], block_sum, IDENTITY, bias=b_tile[:, m : m + 1])


def dense_layer(nc, sums, w_tile, b_tile, h_in, h_out, on_vector):
    banks = open_banks(sums, w_tile, h_in.shape[2])
    for j in range(w_tile.shape[1]):
        add_block(nc, banks, w_tile, h_in, j)
    add_bias(nc, h_out, banks, b_tile, on_vector)


def tile_lcnspiking_b_kernel(tc, x, w0, b0, w1, b1, w2, b2, w3, b3, w4, b4, fc_w, fc_b, offs, out):
    nc = tc.nc
    with (
        tc.tile_pool(name="held", bufs=1) as held,
        tc.tile_pool(name="acts", bufs=2) as acts,
        tc.psum_pool(name="flipped", bufs=3) as flipped,
        tc.psum_pool(name="sums", bufs=5) as sums,
    ):
        w0_rows = held.tile([N // P, P], F32, name="w0_rows")
        nc.sync.dma_start(w0_rows[:], w0.rearrange("o (q n) -> (o q) n", n=P))
        offsets = held.tile([P, N // 16], U16, name="offsets")
        nc.sync.dma_start(offsets[:], offs)

        w0_spread = held.tile([P, KN, D1], F32, name="w0_spread")
        x_blocks = [held.tile([P, S], F32, name="x_block%d" % b) for b in range(SAMPLE_BLOCKS)]

        w1_tile = weight_tile(held, "w1_tile", w1)
        w2_tile = weight_tile(held, "w2_tile", w2)
        w3_tile = weight_tile(held, "w3_tile", w3)
        w4_tile = weight_tile(held, "w4_tile", w4)
        fcw_tile = weight_tile(held, "fcw_tile", fc_w)

        nc.sync.dma_start(x_blocks[0][:], x[0:P, :])
        biases = [b0, b1, b2, b3, b4, fc_b]
        bias_rows = held.tile([P, P], F32, name="bias_rows")
        nc.gpsimd.memset(bias_rows[:], 0.0)
        load_bias_rows(nc, bias_rows, biases)
        load_blocks(nc, w1_tile, w1, 0, 4)
        load_blocks(nc, w1_tile, w1, 4, 8)
        nc.sync.dma_start(x_blocks[1][:], x[P : 2 * P, :])
        load_blocks(nc, w1_tile, w1, 8, 12)
        load_blocks(nc, w1_tile, w1, 12, 16)
        load_blocks(nc, w2_tile, w2, 0, D2 // P)
        load_blocks(nc, w3_tile, w3, 0, D3 // P)
        load_blocks(nc, w4_tile, w4, 0, D4 // P)
        load_blocks(nc, fcw_tile, fc_w, 0, D5 // P)
        nc.sync.dma_start(x_blocks[2][:], x[2 * P : 3 * P, :])

        identity = held.tile([P, P], F32, name="identity")
        make_identity(nc, identity[:])

        w0_columns = turn_rows(nc, held, flipped, identity, "w0_columns", w0_rows)
        for d in range(0, D1, BANK):
            for k in range(KN):
                spread(nc, flipped, identity, w0_columns, (k * D1 + d) // P, w0_spread[:, k, d : d + BANK])

        bias_columns = turn_rows(nc, held, flipped, identity, "bias_columns", bias_rows)
        first_column = [sum(b.shape[0] // P for b in biases[:i]) for i in range(len(biases))]
        b0_tile, b1_tile, b2_tile, b3_tile, b4_tile = [
            bias_columns[:, first : first + b.shape[0] // P] for first, b in zip(first_column[:-1], biases[:-1])
        ]
        fcb_column = bias_columns[:, first_column[-1] : first_column[-1] + 1]

        h2_blocks = [held.tile([P, D3 // P, P], BF16, name="h2_block%d" % b) for b in range(SAMPLE_BLOCKS)]
        h3_blocks = [held.tile([P, D4 // P, P], BF16, name="h3_block%d" % b) for b in range(SAMPLE_BLOCKS)]
        h4_blocks = [held.tile([P, D5 // P, P], BF16, name="h4_block%d" % b) for b in range(SAMPLE_BLOCKS)]

        def third_layer(h1_banks, h2, on_vector):
            h1 = acts.tile([P, D2 // P, P], BF16, name="h1")
            add_bias(nc, h1, h1_banks, b1_tile, on_vector)
            dense_layer(nc, sums, w2_tile, b2_tile, h1, h2, on_vector)

        def read_out(b, h4, on_vector):
            out_sum = sums.tile([P, BANK_BLOCKS, P], F32, name="acc")
            nc.tensor.matmul(
                out_sum[:, 0, :], lhsT=fcb_column.to_broadcast([P, P]), rhs=identity[:], is_transpose=True, start=True, stop=False
            )
            nc.tensor.matmul(out_sum[:, 0, :], lhsT=h4, rhs=fcw_tile[:, 0, :], start=False, stop=True)
            out_rows = held.tile([P, OUT], F32, name="out_rows%d" % b)
            if on_vector:
                nc.vector.tensor_copy(out_rows[:], out_sum[:, 0, :])
            else:
                nc.scalar.activation(out_rows[:], out_sum[:, 0, :], IDENTITY)
            nc.sync.dma_start(out[b * P : (b + 1) * P, :], out_rows[:])

        def second_layer(rounded):
            due, b, begin, y0, h1_banks = rounded
            for i in range(STEP // P):
                add_block(nc, h1_banks, w1_tile, y0, begin // P + i)
            if begin + STEP < D1:
                return
            is_last = b == SAMPLE_BLOCKS - 1
            third_layer(h1_banks, h2_blocks[b], is_last)
            dense_layer(nc, sums, w3_tile, b3_tile, h2_blocks[b], h3_blocks[b], is_last)
            dense_layer(nc, sums, w4_tile, b4_tile, h3_blocks[b], h4_blocks[b], is_last)
            read_out(b, h4_blocks[b][:, 0, :], is_last)

        waiting = []
        steps = 0
        prod = held.tile([P, KN, D1], F32, name="prod")
        for b in range(SAMPLE_BLOCKS):
            y0 = acts.tile([P, D1 // P, P], BF16, name="y0")
            h1_banks = open_banks(sums, w1_tile, P)
            if b == SAMPLE_BLOCKS - 1:
                cuts = staggered_cuts(0, D1 - PLAIN_END) + plain_cuts(D1 - PLAIN_END, D1)
            else:
                cuts = staggered_cuts(0, D1)
            for k, first, last, begin, step_ends in cuts:
                nc.vector.tensor_tensor(
                    prod[:, k, first:last],
                    x_blocks[b][:].indirect(offsets[:, (k * D1 + first) // 16 : (k * D1 + last) // 16]),
                    w0_spread[:, k, first:last],
                    MULT,
                )
                if begin is not None:
                    y0_sum = flipped.tile([P, BANK_BLOCKS, P], F32, name="y0_sum", tag="bank")
                    for turn in range(1, KN + 1):
                        for i in range(STEP // P):
                            nc.tensor.matmul(
                                y0_sum[:, i, :],
                                lhsT=prod[:, (k + turn) % KN, begin + i * P : begin + (i + 1) * P],
                                rhs=identity[:],
                                is_transpose=True,
                                start=(turn == 1 and i == 0),
                                stop=(turn == KN and i == STEP // P - 1),
                            )
                if step_ends:
                    steps += 1
                    if waiting and waiting[0][0] <= steps:
                        second_layer(waiting[0])
                        waiting = waiting[1:]
                if begin is not None:
                    very_last = b == SAMPLE_BLOCKS - 1 and begin + STEP == D1
                    for i in range(STEP // P):
                        j = begin // P + i
                        if very_last:
                            nc.vector.tensor_scalar_add(y0[:, j, :], y0_sum[:, i, :], b0_tile[:, j : j + 1])
                        else:
                            nc.scalar.activation(y0[:, j, :], y0_sum[:, i, :], IDENTITY, bias=b0_tile[:, j : j + 1])
                    waiting.append((steps + LAG, b, begin, y0, h1_banks))
        for rounded in waiting:
            second_layer(rounded)
